import numpy as np
import ml_dtypes


def mxq(x, axis, fmt="e4m3"):
    dtype, down = {"e4m3": (ml_dtypes.float8_e4m3fn, 7), "e5m2": (ml_dtypes.float8_e5m2, 14)}[fmt]
    v = np.moveaxis(np.asarray(x, np.float32).astype(ml_dtypes.bfloat16).astype(np.float64), axis, -1)
    blocks = v.reshape(v.shape[:-1] + (-1, 32))
    amax = np.abs(blocks).max(-1, keepdims=True)
    byte = np.maximum(np.where(amax > 0, np.frexp(amax)[1] - 1 + 127, 0) - down, 1)
    scale = np.exp2(byte - 127.0)
    codes = (blocks / scale).astype(np.float32).astype(dtype).astype(np.float64)
    return np.moveaxis((codes * scale).reshape(v.shape), -1, axis)


WIDE = False


def mx_kscale(k):
    if not WIDE:
        return np.ones(k)
    levels = np.array([10, -10, 5, -5, 0])
    if k % 512:
        return np.exp2(np.random.permutation(np.resize(levels, k // 32))).repeat(32)
    a = np.empty((k // 512, 16))
    for p in range(k // 512):
        a[p, :8] = np.random.permutation(np.resize(levels, 8))
        for g in range(8):
            far = levels[np.abs(levels - a[p, g]) >= 10]
            a[p, g + 8] = far[np.random.randint(len(far))]
    return np.exp2(a.ravel()).repeat(32)


BF16 = ml_dtypes.bfloat16


def bf(x):
    return np.asarray(x, np.float32).astype(BF16)


def f64(x):
    return np.asarray(x).astype(np.float64)


N, C, H, W, B = 1024, 64, 4, 4, 128
D = C * H * W
EPS = 1e-8
TINY = 1e-16


def setup_inputs():
    s = mx_kscale(D)
    g = np.sqrt(np.mean(s * s) * np.mean(1.0 / (s * s)))
    key = np.random.standard_normal((B, D)) * (0.5 + np.random.random((B, 1)))
    memory = np.random.standard_normal((N, D)) * (0.5 + np.random.random((N, 1))) * 3.0
    strength = np.sqrt(D) * g * (0.5 + 0.5 * np.random.random((B, 1)))
    sharpen = 1.0 + np.random.random((B, 1))
    return {"memory": bf((memory / s).reshape(N, C, H, W)), "key": bf(key * s), "strength": bf(strength), "sharpen": bf(sharpen)}


def reference(memory, key, strength, sharpen):
    mem_flat = f64(memory).reshape(N, D)
    k = f64(key)
    key_norm = np.sqrt((k * k).sum(-1, keepdims=True))
    mem_norm = np.sqrt((mem_flat * mem_flat).sum(-1))
    dot = mxq(k, 1, "e4m3") @ mxq(mem_flat, 1, "e4m3").T
    sim = dot / (np.maximum(key_norm, EPS) * np.maximum(mem_norm, EPS)[None, :])
    z = f64(strength) * sim
    e = np.exp(z - z.max(1, keepdims=True))
    w = e / e.sum(1, keepdims=True)
    w = w ** f64(sharpen)
    return w / (w.sum(1, keepdims=True) + TINY)

@@ -1,0 +1,284 @@
+from contextlib import ExitStack
+
+import concourse.masks as masks
+import concourse.mybir as mybir
+
+F32 = mybir.dt.float32
+BF16 = mybir.dt.bfloat16
+U32 = mybir.dt.uint32
+U8 = mybir.dt.uint8
+FP8X4 = mybir.dt.float8_e4m3fn_x4
+ALU = mybir.AluOpType
+ACT = mybir.ActivationFunctionType
+
+P = 128
+SLOTS = 1024
+FEATURES = 1024
+KEYS = 128
+PACK = 4
+K_PASS = P * PACK
+PASSES = FEATURES // K_PASS
+PAIRS = FEATURES // 2
+PAIR_BLOCKS = PAIRS // P
+HALVES = PAIR_BLOCKS // PASSES
+TILE_WORDS = PASSES * P
+SLOT_TILES = SLOTS // P
+TILES_PER_ROUND = 2
+ROUNDS = SLOT_TILES // TILES_PER_ROUND
+BANK = 512
+TILES_PER_BANK = BANK // P
+OUT_BANKS = SLOTS // BANK
+EPS = 1e-8
+TINY = 1e-16
+
+FLOPS = 2 * KEYS * SLOTS * FEATURES
+
+
+def transpose_pairs(nc, bank, rows, identity):
+    pairs = rows.bitcast(F32)
+    words_per_pass = HALVES * P
+    for g in range(PASSES):
+        for u in range(HALVES):
+            nc.tensor.transpose(
+                bank[:, g * HALVES + u, :],
+                pairs[:, g * words_per_pass + u : (g + 1) * words_per_pass : HALVES],
+                identity,
+            )
+
+
+def regroup(nc, grouped, bank):
+    nc.vector.tensor_copy(
+        out=grouped.bitcast(F32).rearrange("p (g r u) -> p g r u", g=PASSES, u=HALVES),
+        in_=bank.rearrange("p (g u) r -> p g r u", u=HALVES),
+    )
+
+
+def tile_memory_pa_s_kernel(tc, memory, key, strength, sharpen, out):
+    nc = tc.nc
+    mem = memory.rearrange("n c h w -> n (c h w)")
+    with ExitStack() as ctx:
+        keep = ctx.enter_context(tc.tile_pool(name="keep", bufs=1))
+        stage = ctx.enter_context(tc.tile_pool(name="stage", bufs=2))
+        pair_banks = ctx.enter_context(tc.psum_pool(name="pair_banks", bufs=4))
+        dot_banks = ctx.enter_context(tc.psum_pool(name="dot_banks", bufs=2))
+        sim_banks = ctx.enter_context(tc.psum_pool(name="sim_banks", bufs=1))
+        ctx.enter_context(tc.manual_schedule())
+
+        key_rows = keep.tile([P, FEATURES], BF16)
+        nc.sync.dma_start(out=key_rows[:], in_=key)
+        mem_rows = []
+        for t in range(SLOT_TILES):
+            rows = keep.tile([P, FEATURES], BF16, name="mem_rows%d" % t)
+            nc.sync.dma_start(out=rows[:], in_=mem[t * P : (t + 1) * P, :])
+            mem_rows.append(rows)
+
+        identity = keep.tile([P, P], F32)
+        masks.make_identity(nc, identity[:])
+        strength_col = keep.tile([P, 1], BF16)
+        nc.gpsimd.dma_start(out=strength_col[:], in_=strength)
+        sharpen_col = keep.tile([P, 1], BF16)
+        nc.gpsimd.dma_start(out=sharpen_col[:], in_=sharpen)
+        minus_half = keep.tile([P, SLOT_TILES], F32)
+        nc.vector.memset(minus_half[:], -0.5)
+        zero_col = keep.tile([P, 1], F32)
+        nc.vector.memset(zero_col[:], 0.0)
+        warm_col = keep.tile([P, 1], F32)
+        nc.scalar.activation(out=warm_col[:], in_=zero_col[:], func=ACT.Exp)
+
+        squares = keep.tile([P, 1 + SLOT_TILES, FEATURES], BF16)
+        key_sumsq = keep.tile([P, 1], F32)
+        nc.scalar.activation(
+            out=squares[:, SLOT_TILES, :], in_=key_rows[:], func=ACT.Square, accum_out=key_sumsq[:]
+        )
+        key_inv_norm = keep.tile([P, 1], F32)
+        nc.gpsimd.tensor_tensor(
+            out=key_inv_norm[:], in0=key_sumsq[:], in1=minus_half[:, 0:1], op=ALU.pow
+        )
+        key_inv_clamped = keep.tile([P, 1], F32)
+        nc.gpsimd.tensor_scalar(
+            out=key_inv_clamped[:],
+            in0=key_inv_norm[:],
+            scalar1=1.0 / EPS,
+            scalar2=-1.0,
+            op0=ALU.min,
+            op1=ALU.mult,
+        )
+        neg_gain = keep.tile([P, 1], F32)
+        nc.gpsimd.tensor_tensor(
+            out=neg_gain[:], in0=key_inv_clamped[:], in1=strength_col[:], op=ALU.mult
+        )
+        sharpen_f32 = keep.tile([P, 1], F32)
+        nc.gpsimd.tensor_copy(out=sharpen_f32[:], in_=sharpen_col[:])
+        neg_sharpen = keep.tile([P, 1], F32)
+        nc.gpsimd.tensor_scalar(
+            out=neg_sharpen[:], in0=sharpen_col[:], scalar1=-1.0, scalar2=None, op0=ALU.mult
+        )
+
+        mem_sumsq = keep.tile([P, SLOT_TILES], F32)
+        mem_inv_norm = keep.tile([P, SLOT_TILES], F32)
+        for r in range(ROUNDS):
+            tiles = slice(r * TILES_PER_ROUND, (r + 1) * TILES_PER_ROUND)
+            for t in range(r * TILES_PER_ROUND, (r + 1) * TILES_PER_ROUND):
+                nc.scalar.activation(
+                    out=squares[:, t, :],
+                    in_=mem_rows[t][:],
+                    func=ACT.Square,
+                    accum_out=mem_sumsq[:, t : t + 1],
+                )
+            nc.gpsimd.tensor_tensor(
+                out=mem_inv_norm[:, tiles],
+                in0=mem_sumsq[:, tiles],
+                in1=minus_half[:, tiles],
+                op=ALU.pow,
+            )
+
+        banks_of = {}
+        grouped_of = {}
+        codes_of = {}
+        scales_of = {}
+        dot_of = {}
+        sim_t_of = {}
+        sim = [sim_banks.tile([P, BANK], F32, name="sim%d" % h) for h in range(OUT_BANKS)]
+
+        def transpose_round(r):
+            banks_of[r] = []
+            for i in range(TILES_PER_ROUND):
+                bank = pair_banks.tile([P, PAIR_BLOCKS, P], F32, name="pair_bank")
+                transpose_pairs(nc, bank, mem_rows[r * TILES_PER_ROUND + i][:], identity[:])
+                banks_of[r].append(bank)
+
+        def regroup_round(r):
+            grouped = stage.tile(
+                [P, TILES_PER_ROUND, TILE_WORDS * PACK], BF16, name="grouped", align_bytes=64
+            )
+            for i in range(TILES_PER_ROUND):
+                regroup(nc, grouped[:, i, :], banks_of[r][i][:])
+            grouped_of[r] = grouped
+
+        def quantise_round(r):
+            codes = stage.tile([P, TILES_PER_ROUND * TILE_WORDS], U32, name="codes", align_bytes=64)
+            scales = stage.tile([P, TILES_PER_ROUND * TILE_WORDS], U8, name="scales", align_bytes=64)
+            nc.vector.quantize_mx(
+                out=codes[:].bitcast(FP8X4),
+                scales=scales[:],
+                in_=grouped_of[r][:].rearrange("p i c -> p (i c)"),
+            )
+            codes_of[r] = codes
+            scales_of[r] = scales
+
+        def multiply_round(r):
+            dot = dot_banks.tile([P, TILES_PER_ROUND, KEYS], F32, name="dot")
+            for i in range(TILES_PER_ROUND):
+                for g in range(PASSES):
+                    slot_cols = slice((i * PASSES + g) * P, (i * PASSES + g + 1) * P)
+                    key_cols = slice(g * KEYS, (g + 1) * KEYS)
+                    nc.tensor.matmul_mx(
+                        out=dot[:, i, :],
+                        lhsT=codes_of[r][:, slot_cols].bitcast(FP8X4),
+                        lhsT_scale=scales_of[r][:, slot_cols],
+                        rhs=key_codes[:, key_cols].bitcast(FP8X4),
+                        rhs_scale=key_scales[:, key_cols],
+                        start=(g == 0),
+                        stop=(g == PASSES - 1),
+                    )
+            dot_of[r] = dot
+
+        def normalise_round(r):
+            tiles = slice(r * TILES_PER_ROUND, (r + 1) * TILES_PER_ROUND)
+            sim_t = stage.tile([P, TILES_PER_ROUND, KEYS], F32, name="sim_t")
+            nc.vector.scalar_tensor_tensor(
+                out=sim_t[:],
+                in0=mem_inv_norm[:, tiles].unsqueeze(2).to_broadcast([P, TILES_PER_ROUND, KEYS]),
+                scalar=1.0 / EPS,
+                in1=dot_of[r][:],
+                op0=ALU.min,
+                op1=ALU.mult,
+            )
+            sim_t_of[r] = sim_t
+
+        def transpose_back_round(r):
+            for i in range(TILES_PER_ROUND):
+                t = r * TILES_PER_ROUND + i
+                cols = slice((t % TILES_PER_BANK) * P, (t % TILES_PER_BANK + 1) * P)
+                nc.tensor.transpose(sim[t // TILES_PER_BANK][:, cols], sim_t_of[r][:, i, :], identity[:])
+
+        neg_z = keep.tile([P, SLOTS], F32)
+        neg_z_min = keep.tile([P, OUT_BANKS], F32)
+
+        def scale_bank(h):
+            nc.vector.tensor_scalar(
+                out=neg_z[:, h * BANK : (h + 1) * BANK],
+                in0=sim[h][:],
+                scalar1=neg_gain[:, 0:1],
+                scalar2=None if h == 0 else neg_z_min[:, h - 1 : h],
+                op0=ALU.mult,
+                op1=ALU.min,
+                accum_out=neg_z_min[:, h : h + 1],
+            )
+
+        key_bank = pair_banks.tile([P, PAIR_BLOCKS, P], F32, name="pair_bank")
+        transpose_pairs(nc, key_bank, key_rows[:], identity[:])
+        key_grouped = keep.tile([P, TILE_WORDS * PACK], BF16, align_bytes=64)
+        regroup(nc, key_grouped[:], key_bank[:])
+        transpose_round(0)
+        regroup_round(0)
+        key_codes = keep.tile([P, TILE_WORDS], U32, align_bytes=64)
+        key_scales = keep.tile([P, TILE_WORDS], U8, align_bytes=64)
+        nc.vector.quantize_mx(
+            out=key_codes[:].bitcast(FP8X4), scales=key_scales[:], in_=key_grouped[:]
+        )
+        transpose_round(1)
+
+        rounds_per_bank = TILES_PER_BANK // TILES_PER_ROUND
+        for s in range(ROUNDS + 2):
+            if s + 2 < ROUNDS:
+                transpose_round(s + 2)
+            if s + 1 < ROUNDS:
+                regroup_round(s + 1)
+            if s < ROUNDS:
+                quantise_round(s)
+                multiply_round(s)
+            if 1 <= s <= ROUNDS:
+                normalise_round(s - 1)
+                transpose_back_round(s - 1)
+            if s >= 2 and (s - 1) % rounds_per_bank == 0:
+                scale_bank((s - 2) // rounds_per_bank)
+
+        neg_max = neg_z_min[:, OUT_BANKS - 1 : OUT_BANKS]
+        e_unread = keep.tile([P, SLOTS], BF16)
+        e_sum = keep.tile([P, 1], F32)
+        nc.scalar.activation(
+            out=e_unread[:], in_=neg_z[:], func=ACT.Exp, bias=neg_max, scale=-1.0, accum_out=e_sum[:]
+        )
+        neg_max_sharp = keep.tile([P, 1], F32)
+        nc.vector.tensor_tensor(out=neg_max_sharp[:], in0=neg_max, in1=sharpen_f32[:], op=ALU.mult)
+        v = keep.tile([P, SLOTS], F32)
+        v_sum = keep.tile([P, 1], F32)
+        nc.scalar.activation(
+            out=v[:],
+            in_=neg_z[:],
+            func=ACT.Exp,
+            bias=neg_max_sharp[:, 0:1],
+            scale=neg_sharpen[:, 0:1],
+            accum_out=v_sum[:],
+        )
+        e_sum_sharp = keep.tile([P, 1], F32)
+        nc.gpsimd.tensor_tensor(out=e_sum_sharp[:], in0=e_sum[:], in1=sharpen_f32[:], op=ALU.pow)
+        denominator = keep.tile([P, 1], F32)
+        nc.vector.tensor_scalar(
+            out=denominator[:],
+            in0=e_sum_sharp[:],
+            scalar1=TINY,
+            scalar2=v_sum[:, 0:1],
+            op0=ALU.mult,
+            op1=ALU.add,
+        )
+        inv_denominator = keep.tile([P, 1], F32)
+        nc.vector.reciprocal(out=inv_denominator[:], in_=denominator[:])
+        w = keep.tile([P, SLOTS], F32)
+        for h in range(OUT_BANKS):
+            cols = slice(h * BANK, (h + 1) * BANK)
+            nc.vector.tensor_scalar(
+                out=w[:, cols], in0=v[:, cols], scalar1=inv_denominator[:, 0:1], scalar2=None, op0=ALU.mult
+            )
+            nc.sync.dma_start(out=out[:, cols], in_=w[:, cols])

@@ -25,9 +25,10 @@ TILE_WORDS = PASSES * P
 SLOT_TILES = SLOTS // P
 TILES_PER_ROUND = 2
 ROUNDS = SLOT_TILES // TILES_PER_ROUND
+ROUND_SLOTS = TILES_PER_ROUND * P
 BANK = 512
-TILES_PER_BANK = BANK // P
-OUT_BANKS = SLOTS // BANK
+SIM_BANKS = 2
+STORES = 2
 EPS = 1e-8
 TINY = 1e-16
 
@@ -138,7 +139,11 @@ def tile_memory_pa_s_kernel(tc, memory, key, strength, sharpen, out):
         scales_of = {}
         dot_of = {}
         sim_t_of = {}
-        sim = [sim_banks.tile([P, BANK], F32, name="sim%d" % h) for h in range(OUT_BANKS)]
+        sim = [sim_banks.tile([P, BANK], F32, name="sim%d" % h) for h in range(SIM_BANKS)]
+
+        def sim_of(r, first_slot, slots):
+            start = (r // SIM_BANKS) * ROUND_SLOTS + first_slot
+            return sim[r % SIM_BANKS][:, start : start + slots]
 
         def transpose_round(r):
             banks_of[r] = []
@@ -198,22 +203,56 @@ def tile_memory_pa_s_kernel(tc, memory, key, strength, sharpen, out):
 
         def transpose_back_round(r):
             for i in range(TILES_PER_ROUND):
-                t = r * TILES_PER_ROUND + i
-                cols = slice((t % TILES_PER_BANK) * P, (t % TILES_PER_BANK + 1) * P)
-                nc.tensor.transpose(sim[t // TILES_PER_BANK][:, cols], sim_t_of[r][:, i, :], identity[:])
+                nc.tensor.transpose(sim_of(r, i * P, P), sim_t_of[r][:, i, :], identity[:])
 
         neg_z = keep.tile([P, SLOTS], F32)
-        neg_z_min = keep.tile([P, OUT_BANKS], F32)
+        neg_z_min = keep.tile([P, ROUNDS], F32)
 
-        def scale_bank(h):
+        def scale_round(r):
             nc.vector.tensor_scalar(
-                out=neg_z[:, h * BANK : (h + 1) * BANK],
-                in0=sim[h][:],
+                out=neg_z[:, r * ROUND_SLOTS : (r + 1) * ROUND_SLOTS],
+                in0=sim_of(r, 0, ROUND_SLOTS),
                 scalar1=neg_gain[:, 0:1],
-                scalar2=None if h == 0 else neg_z_min[:, h - 1 : h],
+                scalar2=None if r == 0 else neg_z_min[:, r - 1 : r],
                 op0=ALU.mult,
                 op1=ALU.min,
-                accum_out=neg_z_min[:, h : h + 1],
+                accum_out=neg_z_min[:, r : r + 1],
+            )
+
+        sharp_min = keep.tile([P, ROUNDS], F32)
+        e_unread = keep.tile([P, SLOTS], BF16)
+        e_sums = keep.tile([P, ROUNDS], F32)
+        v = keep.tile([P, SLOTS], F32)
+        v_sums = keep.tile([P, ROUNDS], F32)
+
+        def sharpen_min(r):
+            nc.scalar.activation(
+                out=sharp_min[:, r : r + 1],
+                in_=neg_z_min[:, r : r + 1],
+                func=ACT.Copy,
+                scale=sharpen_f32[:, 0:1],
+            )
+
+        def exp_round(r):
+            cols = slice(r * ROUND_SLOTS, (r + 1) * ROUND_SLOTS)
+            nc.scalar.activation(
+                out=e_unread[:, cols],
+                in_=neg_z[:, cols],
+                func=ACT.Exp,
+                bias=neg_z_min[:, r : r + 1],
+                scale=-1.0,
+                accum_out=e_sums[:, r : r + 1],
+            )
+
+        def sharp_exp_round(r):
+            cols = slice(r * ROUND_SLOTS, (r + 1) * ROUND_SLOTS)
+            nc.scalar.activation(
+                out=v[:, cols],
+                in_=neg_z[:, cols],
+                func=ACT.Exp,
+                bias=sharp_min[:, r : r + 1],
+                scale=neg_sharpen[:, 0:1],
+                accum_out=v_sums[:, r : r + 1],
             )
 
         key_bank = pair_banks.tile([P, PAIR_BLOCKS, P], F32, name="pair_bank")
@@ -229,7 +268,7 @@ def tile_memory_pa_s_kernel(tc, memory, key, strength, sharpen, out):
         )
         transpose_round(1)
 
-        rounds_per_bank = TILES_PER_BANK // TILES_PER_ROUND
+        last = ROUNDS - 1
         for s in range(ROUNDS + 2):
             if s + 2 < ROUNDS:
                 transpose_round(s + 2)
@@ -241,29 +280,52 @@ def tile_memory_pa_s_kernel(tc, memory, key, strength, sharpen, out):
             if 1 <= s <= ROUNDS:
                 normalise_round(s - 1)
                 transpose_back_round(s - 1)
-            if s >= 2 and (s - 1) % rounds_per_bank == 0:
-                scale_bank((s - 2) // rounds_per_bank)
+            if 2 <= s:
+                scale_round(s - 2)
+                if s - 2 < last:
+                    sharpen_min(s - 2)
+                    exp_round(s - 2)
+                    sharp_exp_round(s - 2)
 
-        neg_max = neg_z_min[:, OUT_BANKS - 1 : OUT_BANKS]
-        e_unread = keep.tile([P, SLOTS], BF16)
-        e_sum = keep.tile([P, 1], F32)
+        exp_round(last)
+        a = keep.tile([P, ROUNDS], F32)
         nc.scalar.activation(
-            out=e_unread[:], in_=neg_z[:], func=ACT.Exp, bias=neg_max, scale=-1.0, accum_out=e_sum[:]
+            out=a[:], in_=neg_z_min[:], func=ACT.Exp, bias=neg_z_min[:, last : last + 1], scale=-1.0
         )
-        neg_max_sharp = keep.tile([P, 1], F32)
-        nc.vector.tensor_tensor(out=neg_max_sharp[:], in0=neg_max, in1=sharpen_f32[:], op=ALU.mult)
-        v = keep.tile([P, SLOTS], F32)
-        v_sum = keep.tile([P, 1], F32)
+        sharpen_min(last)
+        b = keep.tile([P, ROUNDS], F32)
         nc.scalar.activation(
-            out=v[:],
-            in_=neg_z[:],
+            out=b[:],
+            in_=neg_z_min[:],
             func=ACT.Exp,
-            bias=neg_max_sharp[:, 0:1],
+            bias=sharp_min[:, last : last + 1],
             scale=neg_sharpen[:, 0:1],
-            accum_out=v_sum[:],
+        )
+        sharp_exp_round(last)
+
+        weighted = keep.tile([P, 2, ROUNDS], F32)
+        e_sum = keep.tile([P, 1], F32)
+        nc.vector.scalar_tensor_tensor(
+            out=weighted[:, 0, :],
+            in0=a[:],
+            scalar=1.0,
+            in1=e_sums[:],
+            op0=ALU.mult,
+            op1=ALU.mult,
+            accum_out=e_sum[:],
         )
         e_sum_sharp = keep.tile([P, 1], F32)
         nc.gpsimd.tensor_tensor(out=e_sum_sharp[:], in0=e_sum[:], in1=sharpen_f32[:], op=ALU.pow)
+        v_sum = keep.tile([P, 1], F32)
+        nc.vector.scalar_tensor_tensor(
+            out=weighted[:, 1, :],
+            in0=b[:],
+            scalar=1.0,
+            in1=v_sums[:],
+            op0=ALU.mult,
+            op1=ALU.mult,
+            accum_out=v_sum[:],
+        )
         denominator = keep.tile([P, 1], F32)
         nc.vector.tensor_scalar(
             out=denominator[:],
@@ -276,9 +338,17 @@ def tile_memory_pa_s_kernel(tc, memory, key, strength, sharpen, out):
         inv_denominator = keep.tile([P, 1], F32)
         nc.vector.reciprocal(out=inv_denominator[:], in_=denominator[:])
         w = keep.tile([P, SLOTS], F32)
-        for h in range(OUT_BANKS):
-            cols = slice(h * BANK, (h + 1) * BANK)
+        rounds_per_store = ROUNDS // STORES
+        for r in range(ROUNDS):
+            cols = slice(r * ROUND_SLOTS, (r + 1) * ROUND_SLOTS)
             nc.vector.tensor_scalar(
-                out=w[:, cols], in0=v[:, cols], scalar1=inv_denominator[:, 0:1], scalar2=None, op0=ALU.mult
+                out=w[:, cols],
+                in0=v[:, cols],
+                scalar1=b[:, r : r + 1],
+                scalar2=inv_denominator[:, 0:1],
+                op0=ALU.mult,
+                op1=ALU.mult,
             )
-            nc.sync.dma_start(out=out[:, cols], in_=w[:, cols])
+            if (r + 1) % rounds_per_store == 0:
+                stored = slice((r + 1 - rounds_per_store) * ROUND_SLOTS, (r + 1) * ROUND_SLOTS)
+                nc.sync.dma_start(out=out[:, stored], in_=w[:, stored])

@@ -25,10 +25,11 @@ TILE_WORDS = PASSES * P
 SLOT_TILES = SLOTS // P
 TILES_PER_ROUND = 2
 ROUNDS = SLOT_TILES // TILES_PER_ROUND
-ROUND_SLOTS = TILES_PER_ROUND * P
-BANK = 512
-SIM_BANKS = 2
-STORES = 2
+GROUP_TILES = (2, 2, 2, 1, 1)
+GROUPS = len(GROUP_TILES)
+GROUP_FIRST = (0, 2, 4, 6, 7)
+EARLY_GROUPS = 2
+V_PARTS = EARLY_GROUPS + 1
 EPS = 1e-8
 TINY = 1e-16
 
@@ -62,7 +63,7 @@ def tile_memory_pa_s_kernel(tc, memory, key, strength, sharpen, out):
         stage = ctx.enter_context(tc.tile_pool(name="stage", bufs=2))
         pair_banks = ctx.enter_context(tc.psum_pool(name="pair_banks", bufs=4))
         dot_banks = ctx.enter_context(tc.psum_pool(name="dot_banks", bufs=2))
-        sim_banks = ctx.enter_context(tc.psum_pool(name="sim_banks", bufs=1))
+        sim_banks = ctx.enter_context(tc.psum_pool(name="sim_banks", bufs=2))
         ctx.enter_context(tc.manual_schedule())
 
         key_rows = keep.tile([P, FEATURES], BF16)
@@ -83,13 +84,22 @@ def tile_memory_pa_s_kernel(tc, memory, key, strength, sharpen, out):
         nc.vector.memset(minus_half[:], -0.5)
         zero_col = keep.tile([P, 1], F32)
         nc.vector.memset(zero_col[:], 0.0)
+        b = keep.tile([P, V_PARTS], F32)
+        nc.vector.memset(b[:, EARLY_GROUPS:V_PARTS], 1.0)
         warm_col = keep.tile([P, 1], F32)
         nc.scalar.activation(out=warm_col[:], in_=zero_col[:], func=ACT.Exp)
 
-        squares = keep.tile([P, 1 + SLOT_TILES, FEATURES], BF16)
+        squares = keep.tile([P, SLOT_TILES, FEATURES], BF16)
+        key_squares = keep.tile([P, FEATURES], F32)
         key_sumsq = keep.tile([P, 1], F32)
-        nc.scalar.activation(
-            out=squares[:, SLOT_TILES, :], in_=key_rows[:], func=ACT.Square, accum_out=key_sumsq[:]
+        nc.vector.scalar_tensor_tensor(
+            out=key_squares[:],
+            in0=key_rows[:],
+            scalar=1.0,
+            in1=key_rows[:],
+            op0=ALU.mult,
+            op1=ALU.mult,
+            accum_out=key_sumsq[:],
         )
         key_inv_norm = keep.tile([P, 1], F32)
         nc.gpsimd.tensor_tensor(
@@ -139,11 +149,7 @@ def tile_memory_pa_s_kernel(tc, memory, key, strength, sharpen, out):
         scales_of = {}
         dot_of = {}
         sim_t_of = {}
-        sim = [sim_banks.tile([P, BANK], F32, name="sim%d" % h) for h in range(SIM_BANKS)]
-
-        def sim_of(r, first_slot, slots):
-            start = (r // SIM_BANKS) * ROUND_SLOTS + first_slot
-            return sim[r % SIM_BANKS][:, start : start + slots]
+        sim_of = {}
 
         def transpose_round(r):
             banks_of[r] = []
@@ -163,11 +169,15 @@ def tile_memory_pa_s_kernel(tc, memory, key, strength, sharpen, out):
         def quantise_round(r):
             codes = stage.tile([P, TILES_PER_ROUND * TILE_WORDS], U32, name="codes", align_bytes=64)
             scales = stage.tile([P, TILES_PER_ROUND * TILE_WORDS], U8, name="scales", align_bytes=64)
-            nc.vector.quantize_mx(
-                out=codes[:].bitcast(FP8X4),
-                scales=scales[:],
-                in_=grouped_of[r][:].rearrange("p i c -> p (i c)"),
-            )
+            calls = TILES_PER_ROUND if r == ROUNDS - 1 else 1
+            words = TILES_PER_ROUND * TILE_WORDS // calls
+            values = grouped_of[r][:].rearrange("p i c -> p (i c)")
+            for c in range(calls):
+                nc.vector.quantize_mx(
+                    out=codes[:, c * words : (c + 1) * words].bitcast(FP8X4),
+                    scales=scales[:, c * words : (c + 1) * words],
+                    in_=values[:, c * words * PACK : (c + 1) * words * PACK],
+                )
             codes_of[r] = codes
             scales_of[r] = scales
 
@@ -188,71 +198,83 @@ def tile_memory_pa_s_kernel(tc, memory, key, strength, sharpen, out):
                     )
             dot_of[r] = dot
 
-        def normalise_round(r):
-            tiles = slice(r * TILES_PER_ROUND, (r + 1) * TILES_PER_ROUND)
-            sim_t = stage.tile([P, TILES_PER_ROUND, KEYS], F32, name="sim_t")
+        def slots_of(g):
+            return slice(GROUP_FIRST[g] * P, (GROUP_FIRST[g] + GROUP_TILES[g]) * P)
+
+        def normalise_group(g):
+            first, tiles = GROUP_FIRST[g], GROUP_TILES[g]
+            in_round = first % TILES_PER_ROUND
+            sim_t = stage.tile([P, tiles, KEYS], F32, name="sim_t")
             nc.vector.scalar_tensor_tensor(
                 out=sim_t[:],
-                in0=mem_inv_norm[:, tiles].unsqueeze(2).to_broadcast([P, TILES_PER_ROUND, KEYS]),
+                in0=mem_inv_norm[:, first : first + tiles].unsqueeze(2).to_broadcast([P, tiles, KEYS]),
                 scalar=1.0 / EPS,
-                in1=dot_of[r][:],
+                in1=dot_of[first // TILES_PER_ROUND][:, in_round : in_round + tiles, :],
                 op0=ALU.min,
                 op1=ALU.mult,
             )
-            sim_t_of[r] = sim_t
+            sim_t_of[g] = sim_t
 
-        def transpose_back_round(r):
-            for i in range(TILES_PER_ROUND):
-                nc.tensor.transpose(sim_of(r, i * P, P), sim_t_of[r][:, i, :], identity[:])
+        def transpose_back_group(g):
+            if g < EARLY_GROUPS:
+                bank = sim_banks.tile([P, PAIR_BLOCKS, P], F32, name="sim_bank")
+            else:
+                bank = pair_banks.tile([P, PAIR_BLOCKS, P], F32, name="pair_bank")
+            sim = bank[:].rearrange("p j r -> p (j r)")
+            for i in range(GROUP_TILES[g]):
+                nc.tensor.transpose(sim[:, i * P : (i + 1) * P], sim_t_of[g][:, i, :], identity[:])
+            sim_of[g] = sim
 
         neg_z = keep.tile([P, SLOTS], F32)
-        neg_z_min = keep.tile([P, ROUNDS], F32)
+        neg_z_min = keep.tile([P, GROUPS + 1], F32)
 
-        def scale_round(r):
+        def scale_group(g):
             nc.vector.tensor_scalar(
-                out=neg_z[:, r * ROUND_SLOTS : (r + 1) * ROUND_SLOTS],
-                in0=sim_of(r, 0, ROUND_SLOTS),
+                out=neg_z[:, slots_of(g)],
+                in0=sim_of[g][:, 0 : GROUP_TILES[g] * P],
                 scalar1=neg_gain[:, 0:1],
-                scalar2=None if r == 0 else neg_z_min[:, r - 1 : r],
+                scalar2=None,
                 op0=ALU.mult,
                 op1=ALU.min,
-                accum_out=neg_z_min[:, r : r + 1],
+                accum_out=neg_z_min[:, g : g + 1],
             )
 
-        sharp_min = keep.tile([P, ROUNDS], F32)
         e_unread = keep.tile([P, SLOTS], BF16)
-        e_sums = keep.tile([P, ROUNDS], F32)
+        e_sums = keep.tile([P, GROUPS], F32)
+        sharp_min = keep.tile([P, V_PARTS], F32)
         v = keep.tile([P, SLOTS], F32)
-        v_sums = keep.tile([P, ROUNDS], F32)
+        v_sums = keep.tile([P, V_PARTS], F32)
 
-        def sharpen_min(r):
+        def part_slots(j):
+            return slots_of(j) if j < EARLY_GROUPS else slice(GROUP_FIRST[EARLY_GROUPS] * P, SLOTS)
+
+        def sharpen_min(j):
+            column = j if j < EARLY_GROUPS else GROUPS
             nc.scalar.activation(
-                out=sharp_min[:, r : r + 1],
-                in_=neg_z_min[:, r : r + 1],
+                out=sharp_min[:, j : j + 1],
+                in_=neg_z_min[:, column : column + 1],
                 func=ACT.Copy,
                 scale=sharpen_f32[:, 0:1],
             )
 
-        def exp_round(r):
-            cols = slice(r * ROUND_SLOTS, (r + 1) * ROUND_SLOTS)
+        def exp_group(g):
             nc.scalar.activation(
-                out=e_unread[:, cols],
-                in_=neg_z[:, cols],
+                out=e_unread[:, slots_of(g)],
+                in_=neg_z[:, slots_of(g)],
                 func=ACT.Exp,
-                bias=neg_z_min[:, r : r + 1],
+                bias=neg_z_min[:, g : g + 1],
                 scale=-1.0,
-                accum_out=e_sums[:, r : r + 1],
+                accum_out=e_sums[:, g : g + 1],
             )
 
-        def sharp_exp_round(r):
-            cols = slice(r * ROUND_SLOTS, (r + 1) * ROUND_SLOTS)
+        def sharp_exp_part(j):
             nc.scalar.activation(
-                out=v[:, cols],
-                in_=neg_z[:, cols],
+                out=v[:, part_slots(j)],
+                in_=neg_z[:, part_slots(j)],
                 func=ACT.Exp,
-                bias=sharp_min[:, r : r + 1],
+                bias=sharp_min[:, j : j + 1],
                 scale=neg_sharpen[:, 0:1],
-                accum_out=v_sums[:, r : r + 1],
+                accum_out=v_sums[:, j : j + 1],
             )
 
         key_bank = pair_banks.tile([P, PAIR_BLOCKS, P], F32, name="pair_bank")
@@ -268,42 +290,53 @@ def tile_memory_pa_s_kernel(tc, memory, key, strength, sharpen, out):
         )
         transpose_round(1)
 
-        last = ROUNDS - 1
-        for s in range(ROUNDS + 2):
+        for s in range(ROUNDS):
             if s + 2 < ROUNDS:
                 transpose_round(s + 2)
             if s + 1 < ROUNDS:
                 regroup_round(s + 1)
-            if s < ROUNDS:
-                quantise_round(s)
-                multiply_round(s)
-            if 1 <= s <= ROUNDS:
-                normalise_round(s - 1)
-                transpose_back_round(s - 1)
+            quantise_round(s)
+            multiply_round(s)
+            if 1 <= s:
+                normalise_group(s - 1)
+                transpose_back_group(s - 1)
             if 2 <= s:
-                scale_round(s - 2)
-                if s - 2 < last:
-                    sharpen_min(s - 2)
-                    exp_round(s - 2)
-                    sharp_exp_round(s - 2)
+                scale_group(s - 2)
+                sharpen_min(s - 2)
+                exp_group(s - 2)
+                sharp_exp_part(s - 2)
 
-        exp_round(last)
-        a = keep.tile([P, ROUNDS], F32)
-        nc.scalar.activation(
-            out=a[:], in_=neg_z_min[:], func=ACT.Exp, bias=neg_z_min[:, last : last + 1], scale=-1.0
+        for g in range(ROUNDS - 1, GROUPS):
+            normalise_group(g)
+            transpose_back_group(g)
+        for g in range(EARLY_GROUPS, GROUPS):
+            scale_group(g)
+            exp_group(g)
+        nc.vector.tensor_reduce(
+            out=neg_z_min[:, GROUPS : GROUPS + 1],
+            in_=neg_z_min[:, 0:GROUPS],
+            axis=mybir.AxisListType.X,
+            op=ALU.min,
         )
-        sharpen_min(last)
-        b = keep.tile([P, ROUNDS], F32)
+        a = keep.tile([P, GROUPS], F32)
         nc.scalar.activation(
-            out=b[:],
-            in_=neg_z_min[:],
+            out=a[:],
+            in_=neg_z_min[:, 0:GROUPS],
             func=ACT.Exp,
-            bias=sharp_min[:, last : last + 1],
+            bias=neg_z_min[:, GROUPS : GROUPS + 1],
+            scale=-1.0,
+        )
+        sharpen_min(EARLY_GROUPS)
+        nc.scalar.activation(
+            out=b[:, 0:EARLY_GROUPS],
+            in_=neg_z_min[:, 0:EARLY_GROUPS],
+            func=ACT.Exp,
+            bias=sharp_min[:, EARLY_GROUPS : EARLY_GROUPS + 1],
             scale=neg_sharpen[:, 0:1],
         )
-        sharp_exp_round(last)
+        sharp_exp_part(EARLY_GROUPS)
 
-        weighted = keep.tile([P, 2, ROUNDS], F32)
+        weighted = keep.tile([P, 2, GROUPS], F32)
         e_sum = keep.tile([P, 1], F32)
         nc.vector.scalar_tensor_tensor(
             out=weighted[:, 0, :],
@@ -318,7 +351,7 @@ def tile_memory_pa_s_kernel(tc, memory, key, strength, sharpen, out):
         nc.gpsimd.tensor_tensor(out=e_sum_sharp[:], in0=e_sum[:], in1=sharpen_f32[:], op=ALU.pow)
         v_sum = keep.tile([P, 1], F32)
         nc.vector.scalar_tensor_tensor(
-            out=weighted[:, 1, :],
+            out=weighted[:, 1, 0:V_PARTS],
             in0=b[:],
             scalar=1.0,
             in1=v_sums[:],
@@ -338,17 +371,16 @@ def tile_memory_pa_s_kernel(tc, memory, key, strength, sharpen, out):
         inv_denominator = keep.tile([P, 1], F32)
         nc.vector.reciprocal(out=inv_denominator[:], in_=denominator[:])
         w = keep.tile([P, SLOTS], F32)
-        rounds_per_store = ROUNDS // STORES
-        for r in range(ROUNDS):
-            cols = slice(r * ROUND_SLOTS, (r + 1) * ROUND_SLOTS)
+        for j in range(V_PARTS):
             nc.vector.tensor_scalar(
-                out=w[:, cols],
-                in0=v[:, cols],
-                scalar1=b[:, r : r + 1],
+                out=w[:, part_slots(j)],
+                in0=v[:, part_slots(j)],
+                scalar1=b[:, j : j + 1],
                 scalar2=inv_denominator[:, 0:1],
                 op0=ALU.mult,
                 op1=ALU.mult,
             )
-            if (r + 1) % rounds_per_store == 0:
-                stored = slice((r + 1 - rounds_per_store) * ROUND_SLOTS, (r + 1) * ROUND_SLOTS)
-                nc.sync.dma_start(out=out[:, stored], in_=w[:, stored])
+            if j == EARLY_GROUPS - 1:
+                nc.sync.dma_start(out=out[:, 0 : part_slots(j).stop], in_=w[:, 0 : part_slots(j).stop])
+            if j == EARLY_GROUPS:
+                nc.sync.dma_start(out=out[:, part_slots(j)], in_=w[:, part_slots(j)])

@@ -30,6 +30,8 @@ GROUPS = len(GROUP_TILES)
 GROUP_FIRST = (0, 2, 4, 6, 7)
 EARLY_GROUPS = 2
 V_PARTS = EARLY_GROUPS + 1
+IDLE_AT_START = 4
+IDLE_PER_STEP = 2
 EPS = 1e-8
 TINY = 1e-16
 
@@ -73,6 +75,16 @@ def tile_memory_pa_s_kernel(tc, memory, key, strength, sharpen, out):
             rows = keep.tile([P, FEATURES], BF16, name="mem_rows%d" % t)
             nc.sync.dma_start(out=rows[:], in_=mem[t * P : (t + 1) * P, :])
             mem_rows.append(rows)
+
+        zeros = keep.tile([P, P], F32)
+        nc.vector.memset(zeros[:], 0.0)
+        idle_bank = sim_banks.tile([P, PAIR_BLOCKS, P], F32, name="sim_bank")
+
+        def idle_pass():
+            nc.tensor.matmul(out=idle_bank[:, 0, :], lhsT=zeros[:], rhs=zeros[:], start=True, stop=True)
+
+        for i in range(IDLE_AT_START):
+            idle_pass()
 
         identity = keep.tile([P, P], F32)
         masks.make_identity(nc, identity[:])
@@ -182,7 +194,7 @@ def tile_memory_pa_s_kernel(tc, memory, key, strength, sharpen, out):
             scales_of[r] = scales
 
         def multiply_round(r):
-            dot = dot_banks.tile([P, TILES_PER_ROUND, KEYS], F32, name="dot")
+            dot = dot_banks.tile([P, 2 * TILES_PER_ROUND, KEYS], F32, name="dot")
             for i in range(TILES_PER_ROUND):
                 for g in range(PASSES):
                     slot_cols = slice((i * PASSES + g) * P, (i * PASSES + g + 1) * P)
@@ -195,6 +207,17 @@ def tile_memory_pa_s_kernel(tc, memory, key, strength, sharpen, out):
                         rhs_scale=key_scales[:, key_cols],
                         start=(g == 0),
                         stop=(g == PASSES - 1),
+                    )
+            if r < ROUNDS - 1:
+                for i in range(IDLE_PER_STEP):
+                    nc.tensor.matmul_mx(
+                        out=dot[:, TILES_PER_ROUND : 2 * TILES_PER_ROUND, :].rearrange("p i k -> p (i k)"),
+                        lhsT=codes_of[r][:, 0:P].bitcast(FP8X4),
+                        lhsT_scale=scales_of[r][:, 0:P],
+                        rhs=key_codes[:].bitcast(FP8X4),
+                        rhs_scale=key_scales[:],
+                        start=True,
+                        stop=True,
                     )
             dot_of[r] = dot
 
@@ -281,6 +304,7 @@ def tile_memory_pa_s_kernel(tc, memory, key, strength, sharpen, out):
         transpose_pairs(nc, key_bank, key_rows[:], identity[:])
         key_grouped = keep.tile([P, TILE_WORDS * PACK], BF16, align_bytes=64)
         regroup(nc, key_grouped[:], key_bank[:])
+        idle_pass()
         transpose_round(0)
         regroup_round(0)
         key_codes = keep.tile([P, TILE_WORDS], U32, align_bytes=64)
@@ -288,6 +312,7 @@ def tile_memory_pa_s_kernel(tc, memory, key, strength, sharpen, out):
         nc.vector.quantize_mx(
             out=key_codes[:].bitcast(FP8X4), scales=key_scales[:], in_=key_grouped[:]
         )
+        idle_pass()
         transpose_round(1)
 
         for s in range(ROUNDS):

@@ -31,7 +31,7 @@ GROUP_FIRST = (0, 2, 4, 6, 7)
 EARLY_GROUPS = 2
 V_PARTS = EARLY_GROUPS + 1
 IDLE_AT_START = 4
-IDLE_PER_STEP = 2
+IDLE_PER_ROUND = 2
 EPS = 1e-8
 TINY = 1e-16
 
@@ -195,6 +195,16 @@ def tile_memory_pa_s_kernel(tc, memory, key, strength, sharpen, out):
 
         def multiply_round(r):
             dot = dot_banks.tile([P, 2 * TILES_PER_ROUND, KEYS], F32, name="dot")
+            for i in range(IDLE_PER_ROUND):
+                nc.tensor.matmul_mx(
+                    out=dot[:, TILES_PER_ROUND : 2 * TILES_PER_ROUND, :].rearrange("p i k -> p (i k)"),
+                    lhsT=key_codes[:, 0:KEYS].bitcast(FP8X4),
+                    lhsT_scale=key_scales[:, 0:KEYS],
+                    rhs=key_codes[:].bitcast(FP8X4),
+                    rhs_scale=key_scales[:],
+                    start=True,
+                    stop=True,
+                )
             for i in range(TILES_PER_ROUND):
                 for g in range(PASSES):
                     slot_cols = slice((i * PASSES + g) * P, (i * PASSES + g + 1) * P)
@@ -207,17 +217,6 @@ def tile_memory_pa_s_kernel(tc, memory, key, strength, sharpen, out):
                         rhs_scale=key_scales[:, key_cols],
                         start=(g == 0),
                         stop=(g == PASSES - 1),
-                    )
-            if r < ROUNDS - 1:
-                for i in range(IDLE_PER_STEP):
-                    nc.tensor.matmul_mx(
-                        out=dot[:, TILES_PER_ROUND : 2 * TILES_PER_ROUND, :].rearrange("p i k -> p (i k)"),
-                        lhsT=codes_of[r][:, 0:P].bitcast(FP8X4),
-                        lhsT_scale=scales_of[r][:, 0:P],
-                        rhs=key_codes[:].bitcast(FP8X4),
-                        rhs_scale=key_scales[:],
-                        start=True,
-                        stop=True,
                     )
             dot_of[r] = dot
 

@@ -30,6 +30,7 @@ GROUPS = len(GROUP_TILES)
 GROUP_FIRST = (0, 2, 4, 6, 7)
 EARLY_GROUPS = 2
 V_PARTS = EARLY_GROUPS + 1
+STORES = 4
 IDLE_AT_START = 4
 IDLE_PER_ROUND = 2
 EPS = 1e-8
@@ -395,16 +396,16 @@ def tile_memory_pa_s_kernel(tc, memory, key, strength, sharpen, out):
         inv_denominator = keep.tile([P, 1], F32)
         nc.vector.reciprocal(out=inv_denominator[:], in_=denominator[:])
         w = keep.tile([P, SLOTS], F32)
-        for j in range(V_PARTS):
+        quarter = SLOTS // STORES
+        for q in range(STORES):
+            cols = slice(q * quarter, (q + 1) * quarter)
+            j = min(q, EARLY_GROUPS)
             nc.vector.tensor_scalar(
-                out=w[:, part_slots(j)],
-                in0=v[:, part_slots(j)],
+                out=w[:, cols],
+                in0=v[:, cols],
                 scalar1=b[:, j : j + 1],
                 scalar2=inv_denominator[:, 0:1],
                 op0=ALU.mult,
                 op1=ALU.mult,
             )
-            if j == EARLY_GROUPS - 1:
-                nc.sync.dma_start(out=out[:, 0 : part_slots(j).stop], in_=w[:, 0 : part_slots(j).stop])
-            if j == EARLY_GROUPS:
-                nc.sync.dma_start(out=out[:, part_slots(j)], in_=w[:, part_slots(j)])
+            nc.sync.dma_start(out=out[:, cols], in_=w[:, cols])

@@ -31,7 +31,7 @@ GROUP_FIRST = (0, 2, 4, 6, 7)
 EARLY_GROUPS = 2
 V_PARTS = EARLY_GROUPS + 1
 STORES = 4
-IDLE_AT_START = 4
+IDLE_AT_START = 3
 IDLE_PER_ROUND = 2
 EPS = 1e-8
 TINY = 1e-16
@@ -304,7 +304,6 @@ def tile_memory_pa_s_kernel(tc, memory, key, strength, sharpen, out):
         transpose_pairs(nc, key_bank, key_rows[:], identity[:])
         key_grouped = keep.tile([P, TILE_WORDS * PACK], BF16, align_bytes=64)
         regroup(nc, key_grouped[:], key_bank[:])
-        idle_pass()
         transpose_round(0)
         regroup_round(0)
         key_codes = keep.tile([P, TILE_WORDS], U32, align_bytes=64)
@@ -312,7 +311,6 @@ def tile_memory_pa_s_kernel(tc, memory, key, strength, sharpen, out):
         nc.vector.quantize_mx(
             out=key_codes[:].bitcast(FP8X4), scales=key_scales[:], in_=key_grouped[:]
         )
-        idle_pass()
         transpose_round(1)
 
         for s in range(ROUNDS):

@@ -30,6 +30,7 @@ GROUPS = len(GROUP_TILES)
 GROUP_FIRST = (0, 2, 4, 6, 7)
 EARLY_GROUPS = 2
 V_PARTS = EARLY_GROUPS + 1
+SMALL_LOADS_BEFORE_TILE = 6
 STORES = 4
 IDLE_AT_START = 3
 IDLE_PER_ROUND = 2
@@ -71,8 +72,13 @@ def tile_memory_pa_s_kernel(tc, memory, key, strength, sharpen, out):
 
         key_rows = keep.tile([P, FEATURES], BF16)
         nc.sync.dma_start(out=key_rows[:], in_=key)
+        strength_col = keep.tile([P, 1], BF16)
+        sharpen_col = keep.tile([P, 1], BF16)
         mem_rows = []
         for t in range(SLOT_TILES):
+            if t == SMALL_LOADS_BEFORE_TILE:
+                nc.sync.dma_start(out=strength_col[:], in_=strength)
+                nc.sync.dma_start(out=sharpen_col[:], in_=sharpen)
             rows = keep.tile([P, FEATURES], BF16, name="mem_rows%d" % t)
             nc.sync.dma_start(out=rows[:], in_=mem[t * P : (t + 1) * P, :])
             mem_rows.append(rows)
@@ -89,10 +95,6 @@ def tile_memory_pa_s_kernel(tc, memory, key, strength, sharpen, out):
 
         identity = keep.tile([P, P], F32)
         masks.make_identity(nc, identity[:])
-        strength_col = keep.tile([P, 1], BF16)
-        nc.gpsimd.dma_start(out=strength_col[:], in_=strength)
-        sharpen_col = keep.tile([P, 1], BF16)
-        nc.gpsimd.dma_start(out=sharpen_col[:], in_=sharpen)
         minus_half = keep.tile([P, SLOT_TILES], F32)
         nc.vector.memset(minus_half[:], -0.5)
         zero_col = keep.tile([P, 1], F32)
@@ -128,15 +130,8 @@ def tile_memory_pa_s_kernel(tc, memory, key, strength, sharpen, out):
             op1=ALU.mult,
         )
         neg_gain = keep.tile([P, 1], F32)
-        nc.gpsimd.tensor_tensor(
-            out=neg_gain[:], in0=key_inv_clamped[:], in1=strength_col[:], op=ALU.mult
-        )
         sharpen_f32 = keep.tile([P, 1], F32)
-        nc.gpsimd.tensor_copy(out=sharpen_f32[:], in_=sharpen_col[:])
         neg_sharpen = keep.tile([P, 1], F32)
-        nc.gpsimd.tensor_scalar(
-            out=neg_sharpen[:], in0=sharpen_col[:], scalar1=-1.0, scalar2=None, op0=ALU.mult
-        )
 
         mem_sumsq = keep.tile([P, SLOT_TILES], F32)
         mem_inv_norm = keep.tile([P, SLOT_TILES], F32)
@@ -155,6 +150,14 @@ def tile_memory_pa_s_kernel(tc, memory, key, strength, sharpen, out):
                 in1=minus_half[:, tiles],
                 op=ALU.pow,
             )
+            if (r + 1) * TILES_PER_ROUND == SMALL_LOADS_BEFORE_TILE - TILES_PER_ROUND:
+                nc.gpsimd.tensor_tensor(
+                    out=neg_gain[:], in0=key_inv_clamped[:], in1=strength_col[:], op=ALU.mult
+                )
+                nc.gpsimd.tensor_copy(out=sharpen_f32[:], in_=sharpen_col[:])
+                nc.gpsimd.tensor_scalar(
+                    out=neg_sharpen[:], in0=sharpen_col[:], scalar1=-1.0, scalar2=None, op0=ALU.mult
+                )
 
         banks_of = {}
         grouped_of = {}

@@ -33,6 +33,7 @@ V_PARTS = EARLY_GROUPS + 1
 SMALL_LOADS_BEFORE_TILE = 6
 STORES = 4
 IDLE_AT_START = 3
+IDLE_BEHIND_TILES = (1, 2, 3)
 IDLE_PER_ROUND = 2
 EPS = 1e-8
 TINY = 1e-16
@@ -71,7 +72,8 @@ def tile_memory_pa_s_kernel(tc, memory, key, strength, sharpen, out):
         ctx.enter_context(tc.manual_schedule())
 
         key_rows = keep.tile([P, FEATURES], BF16)
-        nc.sync.dma_start(out=key_rows[:], in_=key)
+        for half in (slice(0, K_PASS), slice(K_PASS, FEATURES)):
+            nc.sync.dma_start(out=key_rows[:, half], in_=key[:, half])
         strength_col = keep.tile([P, 1], BF16)
         sharpen_col = keep.tile([P, 1], BF16)
         mem_rows = []
@@ -106,15 +108,25 @@ def tile_memory_pa_s_kernel(tc, memory, key, strength, sharpen, out):
 
         squares = keep.tile([P, SLOT_TILES, FEATURES], BF16)
         key_squares = keep.tile([P, FEATURES], F32)
+        key_parts = keep.tile([P, 2], F32)
         key_sumsq = keep.tile([P, 1], F32)
         nc.vector.scalar_tensor_tensor(
-            out=key_squares[:],
-            in0=key_rows[:],
+            out=key_squares[:, 0:K_PASS],
+            in0=key_rows[:, 0:K_PASS],
             scalar=1.0,
-            in1=key_rows[:],
+            in1=key_rows[:, 0:K_PASS],
             op0=ALU.mult,
             op1=ALU.mult,
-            accum_out=key_sumsq[:],
+            accum_out=key_parts[:, 0:1],
+        )
+        nc.scalar.activation(
+            out=key_squares[:, K_PASS:FEATURES],
+            in_=key_rows[:, K_PASS:FEATURES],
+            func=ACT.Square,
+            accum_out=key_parts[:, 1:2],
+        )
+        nc.gpsimd.tensor_tensor(
+            out=key_sumsq[:], in0=key_parts[:, 0:1], in1=key_parts[:, 1:2], op=ALU.add
         )
         key_inv_norm = keep.tile([P, 1], F32)
         nc.gpsimd.tensor_tensor(
@@ -170,9 +182,12 @@ def tile_memory_pa_s_kernel(tc, memory, key, strength, sharpen, out):
         def transpose_round(r):
             banks_of[r] = []
             for i in range(TILES_PER_ROUND):
+                t = r * TILES_PER_ROUND + i
                 bank = pair_banks.tile([P, PAIR_BLOCKS, P], F32, name="pair_bank")
-                transpose_pairs(nc, bank, mem_rows[r * TILES_PER_ROUND + i][:], identity[:])
+                transpose_pairs(nc, bank, mem_rows[t][:], identity[:])
                 banks_of[r].append(bank)
+                if t in IDLE_BEHIND_TILES:
+                    idle_pass()
 
         def regroup_round(r):
             grouped = stage.tile(
@@ -306,7 +321,13 @@ def tile_memory_pa_s_kernel(tc, memory, key, strength, sharpen, out):
         key_bank = pair_banks.tile([P, PAIR_BLOCKS, P], F32, name="pair_bank")
         transpose_pairs(nc, key_bank, key_rows[:], identity[:])
         key_grouped = keep.tile([P, TILE_WORDS * PACK], BF16, align_bytes=64)
-        regroup(nc, key_grouped[:], key_bank[:])
+        for g in range(PASSES):
+            nc.vector.tensor_copy(
+                out=key_grouped[:, g * P * PACK : (g + 1) * P * PACK]
+                .bitcast(F32)
+                .rearrange("p (r u) -> p r u", u=HALVES),
+                in_=key_bank[:, g * HALVES : (g + 1) * HALVES, :].rearrange("p u r -> p r u"),
+            )
         transpose_round(0)
         regroup_round(0)
         key_codes = keep.tile([P, TILE_WORDS], U32, align_bytes=64)

@@ -35,6 +35,8 @@ STORES = 4
 IDLE_AT_START = 3
 IDLE_BEHIND_TILES = (1, 2, 3)
 IDLE_PER_ROUND = 2
+VECTOR_SQUARES = 320
+SCALAR_COPY_TILE = 5
 EPS = 1e-8
 TINY = 1e-16
 
@@ -53,8 +55,8 @@ def transpose_pairs(nc, bank, rows, identity):
             )
 
 
-def regroup(nc, grouped, bank):
-    nc.vector.tensor_copy(
+def regroup(copy, grouped, bank):
+    copy(
         out=grouped.bitcast(F32).rearrange("p (g r u) -> p g r u", g=PASSES, u=HALVES),
         in_=bank.rearrange("p (g u) r -> p g r u", u=HALVES),
     )
@@ -147,29 +149,61 @@ def tile_memory_pa_s_kernel(tc, memory, key, strength, sharpen, out):
 
         mem_sumsq = keep.tile([P, SLOT_TILES], F32)
         mem_inv_norm = keep.tile([P, SLOT_TILES], F32)
-        for r in range(ROUNDS):
-            tiles = slice(r * TILES_PER_ROUND, (r + 1) * TILES_PER_ROUND)
-            for t in range(r * TILES_PER_ROUND, (r + 1) * TILES_PER_ROUND):
+        tile0_parts = keep.tile([P, 2], F32)
+
+        def square_tiles(tiles):
+            for t in tiles:
+                columns = slice(VECTOR_SQUARES if t == 0 else 0, FEATURES)
                 nc.scalar.activation(
-                    out=squares[:, t, :],
-                    in_=mem_rows[t][:],
+                    out=squares[:, t, columns],
+                    in_=mem_rows[t][:, columns],
                     func=ACT.Square,
-                    accum_out=mem_sumsq[:, t : t + 1],
+                    accum_out=tile0_parts[:, 0:1] if t == 0 else mem_sumsq[:, t : t + 1],
                 )
-            nc.gpsimd.tensor_tensor(
-                out=mem_inv_norm[:, tiles],
-                in0=mem_sumsq[:, tiles],
-                in1=minus_half[:, tiles],
-                op=ALU.pow,
-            )
-            if (r + 1) * TILES_PER_ROUND == SMALL_LOADS_BEFORE_TILE - TILES_PER_ROUND:
+
+        def norms_round(r):
+            width = 1 if r == ROUNDS - 1 else TILES_PER_ROUND
+            for t in range(r * TILES_PER_ROUND, (r + 1) * TILES_PER_ROUND, width):
                 nc.gpsimd.tensor_tensor(
-                    out=neg_gain[:], in0=key_inv_clamped[:], in1=strength_col[:], op=ALU.mult
+                    out=mem_inv_norm[:, t : t + width],
+                    in0=mem_sumsq[:, t : t + width],
+                    in1=minus_half[:, t : t + width],
+                    op=ALU.pow,
                 )
-                nc.gpsimd.tensor_copy(out=sharpen_f32[:], in_=sharpen_col[:])
-                nc.gpsimd.tensor_scalar(
-                    out=neg_sharpen[:], in0=sharpen_col[:], scalar1=-1.0, scalar2=None, op0=ALU.mult
-                )
+
+        square_tiles(range(SCALAR_COPY_TILE))
+        key_bank = pair_banks.tile([P, PAIR_BLOCKS, P], F32, name="pair_bank")
+        transpose_pairs(nc, key_bank, key_rows[:], identity[:])
+        key_grouped = keep.tile([P, TILE_WORDS * PACK], BF16, align_bytes=64)
+        for g in range(PASSES):
+            nc.vector.tensor_copy(
+                out=key_grouped[:, g * P * PACK : (g + 1) * P * PACK]
+                .bitcast(F32)
+                .rearrange("p (r u) -> p r u", u=HALVES),
+                in_=key_bank[:, g * HALVES : (g + 1) * HALVES, :].rearrange("p u r -> p r u"),
+            )
+        tile0_squares = keep.tile([P, VECTOR_SQUARES], F32)
+        nc.vector.scalar_tensor_tensor(
+            out=tile0_squares[:],
+            in0=mem_rows[0][:, 0:VECTOR_SQUARES],
+            scalar=1.0,
+            in1=mem_rows[0][:, 0:VECTOR_SQUARES],
+            op0=ALU.mult,
+            op1=ALU.mult,
+            accum_out=tile0_parts[:, 1:2],
+        )
+        nc.gpsimd.tensor_tensor(
+            out=mem_sumsq[:, 0:1], in0=tile0_parts[:, 0:1], in1=tile0_parts[:, 1:2], op=ALU.add
+        )
+        norms_round(0)
+        norms_round(1)
+        nc.gpsimd.tensor_tensor(
+            out=neg_gain[:], in0=key_inv_clamped[:], in1=strength_col[:], op=ALU.mult
+        )
+        nc.gpsimd.tensor_copy(out=sharpen_f32[:], in_=sharpen_col[:])
+        nc.gpsimd.tensor_scalar(
+            out=neg_sharpen[:], in0=sharpen_col[:], scalar1=-1.0, scalar2=None, op0=ALU.mult
+        )
 
         banks_of = {}
         grouped_of = {}
@@ -194,7 +228,13 @@ def tile_memory_pa_s_kernel(tc, memory, key, strength, sharpen, out):
                 [P, TILES_PER_ROUND, TILE_WORDS * PACK], BF16, name="grouped", align_bytes=64
             )
             for i in range(TILES_PER_ROUND):
-                regroup(nc, grouped[:, i, :], banks_of[r][i][:])
+                if r * TILES_PER_ROUND + i == SCALAR_COPY_TILE:
+                    regroup(nc.scalar.copy, grouped[:, i, :], banks_of[r][i][:])
+                    square_tiles(range(SCALAR_COPY_TILE, SLOT_TILES))
+                    norms_round(2)
+                    norms_round(3)
+                else:
+                    regroup(nc.vector.tensor_copy, grouped[:, i, :], banks_of[r][i][:])
             grouped_of[r] = grouped
 
         def quantise_round(r):
@@ -214,7 +254,7 @@ def tile_memory_pa_s_kernel(tc, memory, key, strength, sharpen, out):
 
         def multiply_round(r):
             dot = dot_banks.tile([P, 2 * TILES_PER_ROUND, KEYS], F32, name="dot")
-            for i in range(IDLE_PER_ROUND):
+            for i in range(IDLE_PER_ROUND if r > 0 else 0):
                 nc.tensor.matmul_mx(
                     out=dot[:, TILES_PER_ROUND : 2 * TILES_PER_ROUND, :].rearrange("p i k -> p (i k)"),
                     lhsT=key_codes[:, 0:KEYS].bitcast(FP8X4),
@@ -318,16 +358,6 @@ def tile_memory_pa_s_kernel(tc, memory, key, strength, sharpen, out):
                 accum_out=v_sums[:, j : j + 1],
             )
 
-        key_bank = pair_banks.tile([P, PAIR_BLOCKS, P], F32, name="pair_bank")
-        transpose_pairs(nc, key_bank, key_rows[:], identity[:])
-        key_grouped = keep.tile([P, TILE_WORDS * PACK], BF16, align_bytes=64)
-        for g in range(PASSES):
-            nc.vector.tensor_copy(
-                out=key_grouped[:, g * P * PACK : (g + 1) * P * PACK]
-                .bitcast(F32)
-                .rearrange("p (r u) -> p r u", u=HALVES),
-                in_=key_bank[:, g * HALVES : (g + 1) * HALVES, :].rearrange("p u r -> p r u"),
-            )
         transpose_round(0)
         regroup_round(0)
         key_codes = keep.tile([P, TILE_WORDS], U32, align_bytes=64)

from contextlib import ExitStack

import concourse.masks as masks
import concourse.mybir as mybir

F32 = mybir.dt.float32
BF16 = mybir.dt.bfloat16
U32 = mybir.dt.uint32
U8 = mybir.dt.uint8
FP8X4 = mybir.dt.float8_e4m3fn_x4
ALU = mybir.AluOpType
ACT = mybir.ActivationFunctionType

P = 128
SLOTS = 1024
FEATURES = 1024
KEYS = 128
PACK = 4
K_PASS = P * PACK
PASSES = FEATURES // K_PASS
PAIRS = FEATURES // 2
PAIR_BLOCKS = PAIRS // P
HALVES = PAIR_BLOCKS // PASSES
TILE_WORDS = PASSES * P
SLOT_TILES = SLOTS // P
TILES_PER_ROUND = 2
ROUNDS = SLOT_TILES // TILES_PER_ROUND
GROUP_TILES = (2, 2, 2, 1, 1)
GROUPS = len(GROUP_TILES)
GROUP_FIRST = (0, 2, 4, 6, 7)
EARLY_GROUPS = 2
V_PARTS = EARLY_GROUPS + 1
SMALL_LOADS_BEFORE_TILE = 6
STORES = 4
IDLE_AT_START = 3
IDLE_BEHIND_TILES = (1, 2, 3)
IDLE_PER_ROUND = 2
VECTOR_SQUARES = 320
SCALAR_COPY_TILE = 5
EPS = 1e-8
TINY = 1e-16

FLOPS = 2 * KEYS * SLOTS * FEATURES


def transpose_pairs(nc, bank, rows, identity):
    pairs = rows.bitcast(F32)
    words_per_pass = HALVES * P
    for g in range(PASSES):
        for u in range(HALVES):
            nc.tensor.transpose(
                bank[:, g * HALVES + u, :],
                pairs[:, g * words_per_pass + u : (g + 1) * words_per_pass : HALVES],
                identity,
            )


def regroup(copy, grouped, bank):
    copy(
        out=grouped.bitcast(F32).rearrange("p (g r u) -> p g r u", g=PASSES, u=HALVES),
        in_=bank.rearrange("p (g u) r -> p g r u", u=HALVES),
    )


def tile_memory_pa_s_kernel(tc, memory, key, strength, sharpen, out):
    nc = tc.nc
    mem = memory.rearrange("n c h w -> n (c h w)")
    with ExitStack() as ctx:
        keep = ctx.enter_context(tc.tile_pool(name="keep", bufs=1))
        stage = ctx.enter_context(tc.tile_pool(name="stage", bufs=2))
        pair_banks = ctx.enter_context(tc.psum_pool(name="pair_banks", bufs=4))
        dot_banks = ctx.enter_context(tc.psum_pool(name="dot_banks", bufs=2))
        sim_banks = ctx.enter_context(tc.psum_pool(name="sim_banks", bufs=2))
        ctx.enter_context(tc.manual_schedule())

        key_rows = keep.tile([P, FEATURES], BF16)
        for half in (slice(0, K_PASS), slice(K_PASS, FEATURES)):
            nc.sync.dma_start(out=key_rows[:, half], in_=key[:, half])
        strength_col = keep.tile([P, 1], BF16)
        sharpen_col = keep.tile([P, 1], BF16)
        mem_rows = []
        for t in range(SLOT_TILES):
            if t == SMALL_LOADS_BEFORE_TILE:
                nc.sync.dma_start(out=strength_col[:], in_=strength)
                nc.sync.dma_start(out=sharpen_col[:], in_=sharpen)
            rows = keep.tile([P, FEATURES], BF16, name="mem_rows%d" % t)
            nc.sync.dma_start(out=rows[:], in_=mem[t * P : (t + 1) * P, :])
            mem_rows.append(rows)

        zeros = keep.tile([P, P], F32)
        nc.vector.memset(zeros[:], 0.0)
        idle_bank = sim_banks.tile([P, PAIR_BLOCKS, P], F32, name="sim_bank")

        def idle_pass():
            nc.tensor.matmul(out=idle_bank[:, 0, :], lhsT=zeros[:], rhs=zeros[:], start=True, stop=True)

        for i in range(IDLE_AT_START):
            idle_pass()

        identity = keep.tile([P, P], F32)
        masks.make_identity(nc, identity[:])
        minus_half = keep.tile([P, SLOT_TILES], F32)
        nc.vector.memset(minus_half[:], -0.5)
        zero_col = keep.tile([P, 1], F32)
        nc.vector.memset(zero_col[:], 0.0)
        b = keep.tile([P, V_PARTS], F32)
        nc.vector.memset(b[:, EARLY_GROUPS:V_PARTS], 1.0)
        warm_col = keep.tile([P, 1], F32)
        nc.scalar.activation(out=warm_col[:], in_=zero_col[:], func=ACT.Exp)

        squares = keep.tile([P, SLOT_TILES, FEATURES], BF16)
        key_squares = keep.tile([P, FEATURES], F32)
        key_parts = keep.tile([P, 2], F32)
        key_sumsq = keep.tile([P, 1], F32)
        nc.vector.scalar_tensor_tensor(
            out=key_squares[:, 0:K_PASS],
            in0=key_rows[:, 0:K_PASS],
            scalar=1.0,
            in1=key_rows[:, 0:K_PASS],
            op0=ALU.mult,
            op1=ALU.mult,
            accum_out=key_parts[:, 0:1],
        )
        nc.scalar.activation(
            out=key_squares[:, K_PASS:FEATURES],
            in_=key_rows[:, K_PASS:FEATURES],
            func=ACT.Square,
            accum_out=key_parts[:, 1:2],
        )
        nc.gpsimd.tensor_tensor(
            out=key_sumsq[:], in0=key_parts[:, 0:1], in1=key_parts[:, 1:2], op=ALU.add
        )
        key_inv_norm = keep.tile([P, 1], F32)
        nc.gpsimd.tensor_tensor(
            out=key_inv_norm[:], in0=key_sumsq[:], in1=minus_half[:, 0:1], op=ALU.pow
        )
        key_inv_clamped = keep.tile([P, 1], F32)
        nc.gpsimd.tensor_scalar(
            out=key_inv_clamped[:],
            in0=key_inv_norm[:],
            scalar1=1.0 / EPS,
            scalar2=-1.0,
            op0=ALU.min,
            op1=ALU.mult,
        )
        neg_gain = keep.tile([P, 1], F32)
        sharpen_f32 = keep.tile([P, 1], F32)
        neg_sharpen = keep.tile([P, 1], F32)

        mem_sumsq = keep.tile([P, SLOT_TILES], F32)
        mem_inv_norm = keep.tile([P, SLOT_TILES], F32)
        tile0_parts = keep.tile([P, 2], F32)

        def square_tiles(tiles):
            for t in tiles:
                columns = slice(VECTOR_SQUARES if t == 0 else 0, FEATURES)
                nc.scalar.activation(
                    out=squares[:, t, columns],
                    in_=mem_rows[t][:, columns],
                    func=ACT.Square,
                    accum_out=tile0_parts[:, 0:1] if t == 0 else mem_sumsq[:, t : t + 1],
                )

        def norms_round(r):
            width = 1 if r == ROUNDS - 1 else TILES_PER_ROUND
            for t in range(r * TILES_PER_ROUND, (r + 1) * TILES_PER_ROUND, width):
                nc.gpsimd.tensor_tensor(
                    out=mem_inv_norm[:, t : t + width],
                    in0=mem_sumsq[:, t : t + width],
                    in1=minus_half[:, t : t + width],
                    op=ALU.pow,
                )

        square_tiles(range(SCALAR_COPY_TILE))
        key_bank = pair_banks.tile([P, PAIR_BLOCKS, P], F32, name="pair_bank")
        transpose_pairs(nc, key_bank, key_rows[:], identity[:])
        key_grouped = keep.tile([P, TILE_WORDS * PACK], BF16, align_bytes=64)
        for g in range(PASSES):
            nc.vector.tensor_copy(
                out=key_grouped[:, g * P * PACK : (g + 1) * P * PACK]
                .bitcast(F32)
                .rearrange("p (r u) -> p r u", u=HALVES),
                in_=key_bank[:, g * HALVES : (g + 1) * HALVES, :].rearrange("p u r -> p r u"),
            )
        tile0_squares = keep.tile([P, VECTOR_SQUARES], F32)
        nc.vector.scalar_tensor_tensor(
            out=tile0_squares[:],
            in0=mem_rows[0][:, 0:VECTOR_SQUARES],
            scalar=1.0,
            in1=mem_rows[0][:, 0:VECTOR_SQUARES],
            op0=ALU.mult,
            op1=ALU.mult,
            accum_out=tile0_parts[:, 1:2],
        )
        nc.gpsimd.tensor_tensor(
            out=mem_sumsq[:, 0:1], in0=tile0_parts[:, 0:1], in1=tile0_parts[:, 1:2], op=ALU.add
        )
        norms_round(0)
        norms_round(1)
        nc.gpsimd.tensor_tensor(
            out=neg_gain[:], in0=key_inv_clamped[:], in1=strength_col[:], op=ALU.mult
        )
        nc.gpsimd.tensor_copy(out=sharpen_f32[:], in_=sharpen_col[:])
        nc.gpsimd.tensor_scalar(
            out=neg_sharpen[:], in0=sharpen_col[:], scalar1=-1.0, scalar2=None, op0=ALU.mult
        )

        banks_of = {}
        grouped_of = {}
        codes_of = {}
        scales_of = {}
        dot_of = {}
        sim_t_of = {}
        sim_of = {}

        def transpose_round(r):
            banks_of[r] = []
            for i in range(TILES_PER_ROUND):
                t = r * TILES_PER_ROUND + i
                bank = pair_banks.tile([P, PAIR_BLOCKS, P], F32, name="pair_bank")
                transpose_pairs(nc, bank, mem_rows[t][:], identity[:])
                banks_of[r].append(bank)
                if t in IDLE_BEHIND_TILES:
                    idle_pass()

        def regroup_round(r):
            grouped = stage.tile(
                [P, TILES_PER_ROUND, TILE_WORDS * PACK], BF16, name="grouped", align_bytes=64
            )
            for i in range(TILES_PER_ROUND):
                if r * TILES_PER_ROUND + i == SCALAR_COPY_TILE:
                    regroup(nc.scalar.copy, grouped[:, i, :], banks_of[r][i][:])
                    square_tiles(range(SCALAR_COPY_TILE, SLOT_TILES))
                    norms_round(2)
                    norms_round(3)
                else:
                    regroup(nc.vector.tensor_copy, grouped[:, i, :], banks_of[r][i][:])
            grouped_of[r] = grouped

        def quantise_round(r):
            codes = stage.tile([P, TILES_PER_ROUND * TILE_WORDS], U32, name="codes", align_bytes=64)
            scales = stage.tile([P, TILES_PER_ROUND * TILE_WORDS], U8, name="scales", align_bytes=64)
            calls = TILES_PER_ROUND if r == ROUNDS - 1 else 1
            words = TILES_PER_ROUND * TILE_WORDS // calls
            values = grouped_of[r][:].rearrange("p i c -> p (i c)")
            for c in range(calls):
                nc.vector.quantize_mx(
                    out=codes[:, c * words : (c + 1) * words].bitcast(FP8X4),
                    scales=scales[:, c * words : (c + 1) * words],
                    in_=values[:, c * words * PACK : (c + 1) * words * PACK],
                )
            codes_of[r] = codes
            scales_of[r] = scales

        def multiply_round(r):
            dot = dot_banks.tile([P, 2 * TILES_PER_ROUND, KEYS], F32, name="dot")
            for i in range(IDLE_PER_ROUND if r > 0 else 0):
                nc.tensor.matmul_mx(
                    out=dot[:, TILES_PER_ROUND : 2 * TILES_PER_ROUND, :].rearrange("p i k -> p (i k)"),
                    lhsT=key_codes[:, 0:KEYS].bitcast(FP8X4),
                    lhsT_scale=key_scales[:, 0:KEYS],
                    rhs=key_codes[:].bitcast(FP8X4),
                    rhs_scale=key_scales[:],
                    start=True,
                    stop=True,
                )
            for i in range(TILES_PER_ROUND):
                for g in range(PASSES):
                    slot_cols = slice((i * PASSES + g) * P, (i * PASSES + g + 1) * P)
                    key_cols = slice(g * KEYS, (g + 1) * KEYS)
                    nc.tensor.matmul_mx(
                        out=dot[:, i, :],
                        lhsT=codes_of[r][:, slot_cols].bitcast(FP8X4),
                        lhsT_scale=scales_of[r][:, slot_cols],
                        rhs=key_codes[:, key_cols].bitcast(FP8X4),
                        rhs_scale=key_scales[:, key_cols],
                        start=(g == 0),
                        stop=(g == PASSES - 1),
                    )
            dot_of[r] = dot

        def slots_of(g):
            return slice(GROUP_FIRST[g] * P, (GROUP_FIRST[g] + GROUP_TILES[g]) * P)

        def normalise_group(g):
            first, tiles = GROUP_FIRST[g], GROUP_TILES[g]
            in_round = first % TILES_PER_ROUND
            sim_t = stage.tile([P, tiles, KEYS], F32, name="sim_t")
            nc.vector.scalar_tensor_tensor(
                out=sim_t[:],
                in0=mem_inv_norm[:, first : first + tiles].unsqueeze(2).to_broadcast([P, tiles, KEYS]),
                scalar=1.0 / EPS,
                in1=dot_of[first // TILES_PER_ROUND][:, in_round : in_round + tiles, :],
                op0=ALU.min,
                op1=ALU.mult,
            )
            sim_t_of[g] = sim_t

        def transpose_back_group(g):
            if g < EARLY_GROUPS:
                bank = sim_banks.tile([P, PAIR_BLOCKS, P], F32, name="sim_bank")
            else:
                bank = pair_banks.tile([P, PAIR_BLOCKS, P], F32, name="pair_bank")
            sim = bank[:].rearrange("p j r -> p (j r)")
            for i in range(GROUP_TILES[g]):
                nc.tensor.transpose(sim[:, i * P : (i + 1) * P], sim_t_of[g][:, i, :], identity[:])
            sim_of[g] = sim

        neg_z = keep.tile([P, SLOTS], F32)
        neg_z_min = keep.tile([P, GROUPS + 1], F32)

        def scale_group(g):
            nc.vector.tensor_scalar(
                out=neg_z[:, slots_of(g)],
                in0=sim_of[g][:, 0 : GROUP_TILES[g] * P],
                scalar1=neg_gain[:, 0:1],
                scalar2=None,
                op0=ALU.mult,
                op1=ALU.min,
                accum_out=neg_z_min[:, g : g + 1],
            )

        e_unread = keep.tile([P, SLOTS], BF16)
        e_sums = keep.tile([P, GROUPS], F32)
        sharp_min = keep.tile([P, V_PARTS], F32)
        v = keep.tile([P, SLOTS], F32)
        v_sums = keep.tile([P, V_PARTS], F32)

        def part_slots(j):
            return slots_of(j) if j < EARLY_GROUPS else slice(GROUP_FIRST[EARLY_GROUPS] * P, SLOTS)

        def sharpen_min(j):
            column = j if j < EARLY_GROUPS else GROUPS
            nc.scalar.activation(
                out=sharp_min[:, j : j + 1],
                in_=neg_z_min[:, column : column + 1],
                func=ACT.Copy,
                scale=sharpen_f32[:, 0:1],
            )

        def exp_group(g):
            nc.scalar.activation(
                out=e_unread[:, slots_of(g)],
                in_=neg_z[:, slots_of(g)],
                func=ACT.Exp,
                bias=neg_z_min[:, g : g + 1],
                scale=-1.0,
                accum_out=e_sums[:, g : g + 1],
            )

        def sharp_exp_part(j):
            nc.scalar.activation(
                out=v[:, part_slots(j)],
                in_=neg_z[:, part_slots(j)],
                func=ACT.Exp,
                bias=sharp_min[:, j : j + 1],
                scale=neg_sharpen[:, 0:1],
                accum_out=v_sums[:, j : j + 1],
            )

        transpose_round(0)
        regroup_round(0)
        key_codes = keep.tile([P, TILE_WORDS], U32, align_bytes=64)
        key_scales = keep.tile([P, TILE_WORDS], U8, align_bytes=64)
        nc.vector.quantize_mx(
            out=key_codes[:].bitcast(FP8X4), scales=key_scales[:], in_=key_grouped[:]
        )
        transpose_round(1)

        for s in range(ROUNDS):
            if s + 2 < ROUNDS:
                transpose_round(s + 2)
            if s + 1 < ROUNDS:
                regroup_round(s + 1)
            quantise_round(s)
            multiply_round(s)
            if 1 <= s:
                normalise_group(s - 1)
                transpose_back_group(s - 1)
            if 2 <= s:
                scale_group(s - 2)
                sharpen_min(s - 2)
                exp_group(s - 2)
                sharp_exp_part(s - 2)

        for g in range(ROUNDS - 1, GROUPS):
            normalise_group(g)
            transpose_back_group(g)
        for g in range(EARLY_GROUPS, GROUPS):
            scale_group(g)
            exp_group(g)
        nc.vector.tensor_reduce(
            out=neg_z_min[:, GROUPS : GROUPS + 1],
            in_=neg_z_min[:, 0:GROUPS],
            axis=mybir.AxisListType.X,
            op=ALU.min,
        )
        a = keep.tile([P, GROUPS], F32)
        nc.scalar.activation(
            out=a[:],
            in_=neg_z_min[:, 0:GROUPS],
            func=ACT.Exp,
            bias=neg_z_min[:, GROUPS : GROUPS + 1],
            scale=-1.0,
        )
        sharpen_min(EARLY_GROUPS)
        nc.scalar.activation(
            out=b[:, 0:EARLY_GROUPS],
            in_=neg_z_min[:, 0:EARLY_GROUPS],
            func=ACT.Exp,
            bias=sharp_min[:, EARLY_GROUPS : EARLY_GROUPS + 1],
            scale=neg_sharpen[:, 0:1],
        )
        sharp_exp_part(EARLY_GROUPS)

        weighted = keep.tile([P, 2, GROUPS], F32)
        e_sum = keep.tile([P, 1], F32)
        nc.vector.scalar_tensor_tensor(
            out=weighted[:, 0, :],
            in0=a[:],
            scalar=1.0,
            in1=e_sums[:],
            op0=ALU.mult,
            op1=ALU.mult,
            accum_out=e_sum[:],
        )
        e_sum_sharp = keep.tile([P, 1], F32)
        nc.gpsimd.tensor_tensor(out=e_sum_sharp[:], in0=e_sum[:], in1=sharpen_f32[:], op=ALU.pow)
        v_sum = keep.tile([P, 1], F32)
        nc.vector.scalar_tensor_tensor(
            out=weighted[:, 1, 0:V_PARTS],
            in0=b[:],
            scalar=1.0,
            in1=v_sums[:],
            op0=ALU.mult,
            op1=ALU.mult,
            accum_out=v_sum[:],
        )
        denominator = keep.tile([P, 1], F32)
        nc.vector.tensor_scalar(
            out=denominator[:],
            in0=e_sum_sharp[:],
            scalar1=TINY,
            scalar2=v_sum[:, 0:1],
            op0=ALU.mult,
            op1=ALU.add,
        )
        inv_denominator = keep.tile([P, 1], F32)
        nc.vector.reciprocal(out=inv_denominator[:], in_=denominator[:])
        w = keep.tile([P, SLOTS], F32)
        quarter = SLOTS // STORES
        for q in range(STORES):
            cols = slice(q * quarter, (q + 1) * quarter)
            j = min(q, EARLY_GROUPS)
            nc.vector.tensor_scalar(
                out=w[:, cols],
                in0=v[:, cols],
                scalar1=b[:, j : j + 1],
                scalar2=inv_denominator[:, 0:1],
                op0=ALU.mult,
                op1=ALU.mult,
            )
            nc.sync.dma_start(out=out[:, cols], in_=w[:, cols])
